import numpy as np
import ml_dtypes


def mxq(x, axis, fmt="e4m3"):
    dtype, down = {"e4m3": (ml_dtypes.float8_e4m3fn, 7), "e5m2": (ml_dtypes.float8_e5m2, 14)}[fmt]
    v = np.moveaxis(np.asarray(x, np.float32).astype(ml_dtypes.bfloat16).astype(np.float64), axis, -1)
    blocks = v.reshape(v.shape[:-1] + (-1, 32))
    amax = np.abs(blocks).max(-1, keepdims=True)
    byte = np.maximum(np.where(amax > 0, np.frexp(amax)[1] - 1 + 127, 0) - down, 1)
    scale = np.exp2(byte - 127.0)
    codes = (blocks / scale).astype(np.float32).astype(dtype).astype(np.float64)
    return np.moveaxis((codes * scale).reshape(v.shape), -1, axis)


WIDE = False


def mx_kscale(k):
    if not WIDE:
        return np.ones(k)
    levels = np.array([10, -10, 5, -5, 0])
    if k % 512:
        return np.exp2(np.random.permutation(np.resize(levels, k // 32))).repeat(32)
    a = np.empty((k // 512, 16))
    for p in range(k // 512):
        a[p, :8] = np.random.permutation(np.resize(levels, 8))
        for g in range(8):
            far = levels[np.abs(levels - a[p, g]) >= 10]
            a[p, g + 8] = far[np.random.randint(len(far))]
    return np.exp2(a.ravel()).repeat(32)


BF16 = ml_dtypes.bfloat16


def bf(x):
    return np.asarray(x, np.float32).astype(BF16)


def f64(x):
    return np.asarray(x).astype(np.float64)


E2M1 = np.array([0.0, 0.5, 1.0, 1.5, 2.0, 3.0, 4.0, 6.0, -0.0, -0.5, -1.0, -1.5, -2.0, -3.0, -4.0, -6.0])


def pack_weight(w, fmt):
    k, n = w.shape
    w = f64(bf(w)).reshape(k // 32, 32, n)
    amax = np.abs(w).max(1)
    if fmt == "e4m3":
        byte = np.frexp(amax)[1] - 1 + 127 - 7
    else:
        mant, ex = np.frexp(amax / 6.0)
        byte = np.where(mant > 0.5, ex, ex - 1) + 127
    byte = np.clip(np.where(amax > 0, byte, 1), 1, 254)
    scaled = (w * np.exp2(127.0 - byte)[:, None, :]).reshape(k, n).astype(np.float32)
    by_word = np.ascontiguousarray(scaled.reshape(k // 512, 128, 4, n).transpose(0, 1, 3, 2))
    if fmt == "e4m3":
        words = by_word.astype(ml_dtypes.float8_e4m3fn).view(np.uint8)
    else:
        c = by_word.astype(ml_dtypes.float4_e2m1fn).view(np.uint8) & 0xF
        words = c[..., 0::2] | (c[..., 1::2] << 4)
    return np.ascontiguousarray(words), np.ascontiguousarray(byte.astype(np.uint8).reshape(k // 512, 16, n))


def unpack_weight(words, scales, fmt):
    g, p, n, _ = words.shape
    if fmt == "e4m3":
        vals = np.ascontiguousarray(words).view(ml_dtypes.float8_e4m3fn).astype(np.float64)
    else:
        nib = np.empty((g, p, n, 4), np.uint8)
        nib[..., 0::2] = words & 0xF
        nib[..., 1::2] = words >> 4
        vals = E2M1[nib]
    vals = vals * np.repeat(np.exp2(scales.astype(np.float64) - 127.0), 8, axis=1)[..., None]
    return vals.transpose(0, 1, 3, 2).reshape(g * 512, n)
def pack4(w):
    words, scales = pack_weight(w, "e2m1")
    return words.reshape(words.shape[0], 128, -1), scales


def unpack4(words, scales):
    return unpack_weight(words.reshape(words.shape[0], 128, -1, 2), scales, "e2m1")


B, L, H, G, DEPTH = 64, 64, 1024, 256, 3
EPS = 1e-5


def layernorm(v, g, b):
    mu = v.mean(-1, keepdims=True)
    var = np.square(v - mu).mean(-1, keepdims=True)
    return (v - mu) / np.sqrt(var + EPS) * g + b


def draw0():
    s, t = mx_kscale(H), mx_kscale(H)
    x_nodes = bf(np.random.standard_normal((B, L, H)) * s)
    w1_words, w1_scales = pack4(np.random.standard_normal((H, H)) / np.sqrt(H) / s[:, None])
    b1 = bf(np.random.standard_normal(H) * 0.3)
    gamma = bf((1.0 + 0.1 * np.random.standard_normal(H)) * t)
    beta = bf(0.2 * np.random.standard_normal(H) * t)
    w2_words, w2_scales = pack4(np.random.standard_normal((H, G)) / np.sqrt(H) / t[:, None])
    b2 = bf(np.random.standard_normal(G) * 0.3)
    return {"x_nodes": x_nodes,
            "w1_words": w1_words,
            "w1_scales": w1_scales,
            "b1": b1,
            "gamma": gamma,
            "beta": beta,
            "w2_words": w2_words,
            "w2_scales": w2_scales,
            "b2": b2}


def core(x_nodes, w1_words, w1_scales, b1, gamma, beta, w2_words, w2_scales, b2):
    h = (mxq(f64(x_nodes), 2, "e4m3") @ unpack4(w1_words, w1_scales)) + f64(b1)
    r = np.maximum(layernorm(h, f64(gamma), f64(beta)), 0.0)
    x1 = (mxq(r, 2, "e4m3") @ unpack4(w2_words, w2_scales)) + f64(b2)
    x2 = np.broadcast_to(x1.max(axis=1, keepdims=True), x1.shape)
    return np.concatenate([x1, x2], axis=2)


def e4m3fn_bytes(y):
    return np.clip(np.asarray(y, np.float64), -448.0, 448.0).astype(np.float32).astype(ml_dtypes.float8_e4m3fn).view(np.uint8)


def e4m3fn_values(b):
    return np.asarray(b, np.uint8).view(ml_dtypes.float8_e4m3fn).astype(np.float64)


def setup_inputs():
    d = draw0()
    x0 = np.asarray(d['x_nodes']).astype(np.float64)
    s = (np.max(np.abs(x0), axis=(0, 1), keepdims=True) / 448.0).astype(np.float32)
    out = {}
    for k, v in d.items():
        if k == 'x_nodes':
            out['x_nodes_bytes'] = e4m3fn_bytes(x0 / s.astype(np.float64))
            out['x_nodes_scale'] = s
        else:
            out[k] = v
    return out


def reference(x_nodes_bytes, x_nodes_scale, w1_words, w1_scales, b1, gamma, beta, w2_words, w2_scales, b2):
    return core(e4m3fn_values(x_nodes_bytes) * x_nodes_scale.astype(np.float64), w1_words, w1_scales, b1, gamma, beta, w2_words, w2_scales, b2)

from contextlib import ExitStack

import concourse.mybir as mybir
from concourse.masks import make_identity

F32 = mybir.dt.float32
BF16 = mybir.dt.bfloat16
I32 = mybir.dt.int32
U32 = mybir.dt.uint32
U8 = mybir.dt.uint8
FP8 = mybir.dt.float8_e4m3fn
FP8X4 = mybir.dt.float8_e4m3fn_x4
FP4X4 = mybir.dt.float4_e2m1fn_x4
ALU = mybir.AluOpType
ACT = mybir.ActivationFunctionType
AXIS = mybir.AxisListType

P = 128
TOKENS, H, G = 4096, 1024, 256
EPS = 1e-5
FLOPS = 2 * TOKENS * H * (H + G)

J = 4
BATCH = P * J
NB = TOKENS // BATCH
NT = TOKENS // P
NPOLY = 8


def tile_sub_graph_pa_t_w4_kernel(
    tc, x_bytes, x_scale, w1_words, w1_scales, b1, gamma, beta, w2_words, w2_scales, b2, out
):
    nc = tc.nc
    x_rows = x_bytes.rearrange("b l k -> (b l) k").rearrange("(n p j) k -> n p j k", p=P, j=J)
    out_rows = out.rearrange("b l c -> (b l) c").rearrange("(n p j) c -> n p j c", p=P, j=J)

    with ExitStack() as ctx:
        keep = ctx.enter_context(tc.tile_pool(name="keep", bufs=1))
        work = ctx.enter_context(tc.tile_pool(name="work", bufs=2))
        psum = ctx.enter_context(tc.psum_pool(name="psum", bufs=2))

        xs = keep.tile([P, 8], F32, name="xs")
        ident = keep.tile([P, P], F32, name="ident")
        w1c = keep.tile([P, 2, 2 * H], U8, name="w1c", align_bytes=64)
        w1s = keep.tile([P, 2, H], U8, name="w1s", align_bytes=64)
        w2c = keep.tile([P, 2, 2 * G], U8, name="w2c", align_bytes=64)
        w2s = keep.tile([P, 2, G], U8, name="w2s", align_bytes=64)
        b1r = keep.tile([P, H], BF16, name="b1r")
        b1p = keep.tile([P, H], F32, name="b1p")
        gar = keep.tile([P, 2, 4], BF16, name="gar")
        ber = keep.tile([P, 2, 4], BF16, name="ber")
        gbf = keep.tile([P, 2, 8], F32, name="gbf")
        b2r = keep.tile([P, G], BF16, name="b2r")
        junk = keep.tile([P, H], BF16, name="junk")
        epsb = keep.tile([P, 1], F32, name="epsb")

        T = {}

        def load(n, j0, j1):
            if j0 == 0:
                T["raw", n] = work.tile([P, J, H], U8, name="raw", tag="raw", bufs=3)
            nc.sync.dma_start(out=T["raw", n][:, j0:j1, :], in_=x_rows[n, :, j0:j1, :])

        def widen(i):
            xb = work.tile([P, H], BF16, name="xb", tag="xb", bufs=3)
            T["xb", i] = xb
            nc.gpsimd.tensor_copy(out=xb[:], in_=T["raw", i // J][:, i % J, :].bitcast(FP8))

        def turn_x(i):
            xt = psum.tile([P, 4, P], F32, name="xt", tag="xt", bufs=2)
            T["xt", i] = xt
            words = T["xb", i][:].bitcast(F32)
            for g in range(2):
                for u in range(2):
                    nc.tensor.transpose(xt[:, 2 * g + u, :], words[:, 256 * g + u : 256 * (g + 1) : 2], ident[:])

        def scale_x(i, g):
            if g == 0:
                T["xg", i] = work.tile([P, 2, P, 4], BF16, name="xg", tag="xg", bufs=2, align_bytes=64)
            src = T["xt", i][:].rearrange("p a r -> p (a r)").bitcast(BF16)
            src = src[:, 512 * g : 512 * (g + 1)].rearrange("p (u r e) -> p r u e", u=2, e=2)
            nc.vector.tensor_tensor(
                out=T["xg", i][:, g].rearrange("p r (u e) -> p r u e", e=2),
                in0=src,
                in1=xs[:, 4 * g : 4 * g + 4].rearrange("p (u e) -> p u e", e=2).unsqueeze(1).to_broadcast([P, P, 2, 2]),
                op=ALU.mult,
            )

        def quant_x(i):
            xc = work.tile([P, 2 * P], U32, name="xc", tag="xc", bufs=3, align_bytes=64)
            xcs = work.tile([P, 2 * P], U8, name="xcs", tag="xcs", bufs=3, align_bytes=64)
            T["xc", i] = (xc, xcs)
            nc.vector.quantize_mx(
                out=xc[:].bitcast(FP8X4), scales=xcs[:], in_=T["xg", i][:].rearrange("p g r t -> p (g r t)")
            )

        def mm1(i, hf):
            xc, xcs = T["xc", i]
            h = psum.tile([P, 512], F32, name="h", tag="h", bufs=2)
            T["h", i, hf] = h
            for g in range(2):
                nc.tensor.matmul_mx(
                    out=h[:],
                    lhsT=xc[:, g * P : (g + 1) * P].bitcast(FP8X4),
                    lhsT_scale=xcs[:, g * P : (g + 1) * P],
                    rhs=w1c[:, g, hf * 1024 : (hf + 1) * 1024].bitcast(FP4X4),
                    rhs_scale=w1s[:, g, hf * 512 : (hf + 1) * 512],
                    start=(g == 0),
                    stop=(g == 1),
                )

        def add_b1(i, hf):
            if hf == 0:
                T["hs", i] = work.tile([P, H], F32, name="hs", tag="hs", bufs=12)
                T["st", i] = work.tile([P, 2], F32, name="st", tag="st", bufs=4)
            nc.vector.scalar_tensor_tensor(
                out=T["hs", i][:, hf * 512 : (hf + 1) * 512].rearrange("p (t m) -> p t m", t=4),
                in0=T["h", i, hf][:].rearrange("p (m t) -> p t m", t=4),
                scalar=1.0,
                in1=b1p[:, hf * 512 : (hf + 1) * 512].rearrange("p (t m) -> p t m", t=4),
                op0=ALU.mult,
                op1=ALU.add,
                accum_out=T["st", i][:, hf : hf + 1],
            )

        def neg_mean(i):
            nm = work.tile([P, 1], F32, name="nm", tag="nm", bufs=6)
            T["nm", i] = nm
            st = T["st", i]
            nc.gpsimd.tensor_scalar(
                out=nm[:], in0=st[:, 0:1], scalar1=st[:, 1:2], scalar2=-1.0 / H, op0=ALU.add, op1=ALU.mult
            )

        def square(i):
            ss = work.tile([P, 1], F32, name="ss", tag="ss", bufs=4)
            rs = work.tile([P, 1], F32, name="rs", tag="rs", bufs=6)
            T["rs", i] = rs
            nc.scalar.activation(
                out=junk[:], in_=T["hs", i][:], func=ACT.Square, bias=T["nm", i][:], scale=1.0, accum_out=ss[:]
            )
            nc.scalar.activation(out=rs[:], in_=ss[:], func=ACT.Abs_reciprocal_sqrt, bias=epsb[:], scale=1.0 / H)

        def norm(i):
            hs = T["hs", i]
            nc.gpsimd.tensor_scalar(
                out=hs[:], in0=hs[:], scalar1=T["nm", i][:], scalar2=T["rs", i][:], op0=ALU.add, op1=ALU.mult
            )

        def turn_n(n, q):
            nt = psum.tile([P, J, P], F32, name="nt", tag="nt", bufs=2)
            T["nt", n, q] = nt
            for j in range(J):
                nc.tensor.transpose(nt[:, j, :], T["hs", n * J + j][:, q * P : (q + 1) * P], ident[:])

        def relu(n, q):
            g, t = divmod(q, 4)
            if t == 0:
                T["rp", n, g] = work.tile([P, 4, BATCH], BF16, name="rp", tag="rp", bufs=3)
            nc.scalar.activation(
                out=T["rp", n, g][:, t, :],
                in_=T["nt", n, q][:].rearrange("p j r -> p (j r)"),
                func=ACT.Relu,
                bias=gbf[:, 1, q : q + 1],
                scale=gbf[:, 0, q : q + 1],
            )

        def group_r(n, g, part):
            if part == 0:
                T["rg", n, g] = work.tile([P, BATCH, 4], BF16, name="rg", tag="rg", bufs=2, align_bytes=64)
            c = slice(part * 256, (part + 1) * 256)
            nc.scalar.copy(
                out=T["rg", n, g][:, c, :], in_=T["rp", n, g][:, :, c].rearrange("p t c -> p c t")
            )

        def quant_r(n, g):
            rc = work.tile([P, BATCH], U32, name="rc", tag="rc", bufs=4, align_bytes=64)
            rcs = work.tile([P, BATCH], U8, name="rcs", tag="rcs", bufs=4, align_bytes=64)
            T["rc", n, g] = (rc, rcs)
            nc.vector.quantize_mx(
                out=rc[:].bitcast(FP8X4), scales=rcs[:], in_=T["rg", n, g][:].rearrange("p c t -> p (c t)")
            )

        def mm2(n, jp):
            y = psum.tile([P, 2, G], F32, name="y", tag="y", bufs=2)
            T["y", n, jp] = y
            for jj in range(2):
                j = 2 * jp + jj
                for c in range(2):
                    for g in range(2):
                        rc, rcs = T["rc", n, g]
                        nc.tensor.matmul_mx(
                            out=y[:, jj, c * P : (c + 1) * P],
                            lhsT=rc[:, j * P : (j + 1) * P].bitcast(FP8X4),
                            lhsT_scale=rcs[:, j * P : (j + 1) * P],
                            rhs=w2c[:, g, c * 256 : (c + 1) * 256].bitcast(FP4X4),
                            rhs_scale=w2s[:, g, c * P : (c + 1) * P],
                            start=(g == 0),
                            stop=(g == 1),
                        )

        def add_b2(n, jp):
            if jp == 0:
                T["x1", n] = work.tile([P, J, G], F32, name="x1", tag="x1", bufs=3)
            nc.vector.tensor_tensor(
                out=T["x1", n][:, 2 * jp : 2 * jp + 2, :],
                in0=T["y", n, jp][:],
                in1=b2r[:].unsqueeze(1).to_broadcast([P, 2, G]),
                op=ALU.add,
            )
            if jp == 1:
                nc.sync.dma_start(out=out_rows[n, :, :, 0:G], in_=T["x1", n][:])

        def turn_1(n, c):
            z = psum.tile([P, J, P], F32, name="z", tag="y", bufs=2)
            T["z", n, c] = z
            for j in range(J):
                nc.tensor.transpose(z[:, j, :], T["x1", n][:, j, c * P : (c + 1) * P], ident[:])

        def pool_max(n, c):
            mx = work.tile([P, NPOLY], F32, name="mx", tag="mx", bufs=4)
            T["mx", n, c] = mx
            nc.vector.tensor_reduce(
                out=mx[:],
                in_=T["z", n, c][:].rearrange("p j (b i) -> p b j i", b=NPOLY),
                axis=AXIS.XY,
                op=ALU.max,
            )

        def spread(n, c):
            mb = work.tile([P, NPOLY, 16], F32, name="mb", tag="mb", bufs=4)
            T["mb", n, c] = mb
            nc.gpsimd.tensor_scalar(
                out=mb[:],
                in0=T["mx", n, c][:].unsqueeze(2).to_broadcast([P, NPOLY, 16]),
                scalar1=1.0,
                scalar2=0.0,
                op0=ALU.mult,
                op1=ALU.add,
            )

        def turn_2(n):
            z2 = psum.tile([P, G], F32, name="z2", tag="y", bufs=2)
            T["z2", n] = z2
            for c in range(2):
                nc.tensor.transpose(
                    z2[:, c * P : (c + 1) * P], T["mb", n, c][:].rearrange("p b i -> p (b i)"), ident[:]
                )

        def store_2(n):
            x2 = work.tile([P, G], F32, name="x2", tag="x2", bufs=3)
            nc.scalar.copy(out=x2[:], in_=T["z2", n][:])
            nc.sync.dma_start(out=out_rows[n, :, :, G : 2 * G], in_=x2[:].unsqueeze(1).to_broadcast([P, J, G]))

        with tc.manual_schedule():
            load(0, 0, 1)
            nc.sync.dma_start(out=xs[:], in_=x_scale.rearrange("a o (g p t) -> p (a o g) t", p=P, t=4).rearrange("p g t -> p g t"))
            nc.vector.memset(w1s[:].rearrange("p g n -> p (g n)").bitcast(I32), 0)
            nc.vector.memset(w2s[:].rearrange("p g n -> p (g n)").bitcast(I32), 0)
            nc.vector.memset(epsb[:], EPS)
            make_identity(nc, ident[:])
            load(0, 1, 4)
            for q in range(4):
                nc.sync.dma_start(
                    out=w1s[32 * q : 32 * q + 4, :, :].bitcast(I32),
                    in_=w1_scales[:, 4 * q : 4 * q + 4, :].rearrange("g r n -> r g n").bitcast(I32),
                )
            nc.sync.dma_start(out=w1c[:], in_=w1_words.rearrange("g p n -> p g n"))
            nc.sync.dma_start(out=b1r[:], in_=b1.partition_broadcast(P))
            nc.sync.dma_start(out=gar[:], in_=gamma.rearrange("(g p t) -> p g t", p=P, t=4))
            nc.sync.dma_start(out=ber[:], in_=beta.rearrange("(g p t) -> p g t", p=P, t=4))
            for q in range(4):
                nc.sync.dma_start(
                    out=w2s[32 * q : 32 * q + 4, :, :].bitcast(I32),
                    in_=w2_scales[:, 4 * q : 4 * q + 4, :].rearrange("g r n -> r g n").bitcast(I32),
                )
            nc.sync.dma_start(out=w2c[:], in_=w2_words.rearrange("g p n -> p g n"))
            nc.sync.dma_start(out=b2r[:], in_=b2.partition_broadcast(P))
            load(1, 0, 4)

            def tile_ok(i):
                return 0 <= i < NT

            def batch_at(s, lag):
                n, k = divmod(s - lag, 4)
                return (n, k) if 0 <= n < NB else None

            for s in range(-3, NT + 12):
                if s % J == 0 and 0 <= s and s // J + 2 < NB:
                    load(s // J + 2, 0, J)
                if tile_ok(s + 3):
                    widen(s + 3)
                if tile_ok(s - 1):
                    square(s - 1)
                    norm(s - 1)
                if tile_ok(s):
                    mm1(s, 0)
                if tile_ok(s + 1):
                    scale_x(s + 1, 0)
                if tile_ok(s):
                    mm1(s, 1)
                    if s == 0:
                        nc.vector.tensor_copy(
                            out=b1p[:].rearrange("p (a t m) -> p a t m", a=2, t=4),
                            in_=b1r[:].rearrange("p (a m t) -> p a t m", a=2, t=4),
                        )
                        nc.vector.tensor_copy(out=gbf[:, 0], in_=gar[:].rearrange("p g t -> p (g t)"))
                        nc.vector.tensor_copy(out=gbf[:, 1], in_=ber[:].rearrange("p g t -> p (g t)"))
                    add_b1(s, 0)
                if tile_ok(s + 1):
                    scale_x(s + 1, 1)
                if tile_ok(s):
                    add_b1(s, 1)
                    neg_mean(s)
                if tile_ok(s + 1):
                    quant_x(s + 1)
                at = batch_at(s, 5)
                if at:
                    for q in (2 * at[1], 2 * at[1] + 1):
                        turn_n(at[0], q)
                        relu(at[0], q)
                at = batch_at(s, 7)
                if at:
                    n, k = at
                    group_r(n, k // 2, k % 2)
                at = batch_at(s, 9)
                if at:
                    n, k = at
                    if k == 0:
                        quant_r(n, 0)
                    if k == 2:
                        quant_r(n, 1)
                        mm2(n, 0)
                    if k == 3:
                        mm2(n, 1)
                        add_b2(n, 0)
                        add_b2(n, 1)
                at = batch_at(s, 13)
                if at:
                    n, k = at
                    if k == 0:
                        turn_1(n, 0)
                        turn_1(n, 1)
                        pool_max(n, 0)
                        pool_max(n, 1)
                        spread(n, 0)
                        spread(n, 1)
                    if k == 1:
                        turn_2(n)
                        store_2(n)
                if tile_ok(s + 2):
                    turn_x(s + 2)
